import numpy as np
import ml_dtypes


def mxq(x, axis, fmt="e4m3"):
    dtype, down = {"e4m3": (ml_dtypes.float8_e4m3fn, 7), "e5m2": (ml_dtypes.float8_e5m2, 14)}[fmt]
    v = np.moveaxis(np.asarray(x, np.float32).astype(ml_dtypes.bfloat16).astype(np.float64), axis, -1)
    blocks = v.reshape(v.shape[:-1] + (-1, 32))
    amax = np.abs(blocks).max(-1, keepdims=True)
    byte = np.maximum(np.where(amax > 0, np.frexp(amax)[1] - 1 + 127, 0) - down, 1)
    scale = np.exp2(byte - 127.0)
    codes = (blocks / scale).astype(np.float32).astype(dtype).astype(np.float64)
    return np.moveaxis((codes * scale).reshape(v.shape), -1, axis)


WIDE = False


def mx_kscale(k):
    if not WIDE:
        return np.ones(k)
    levels = np.array([10, -10, 5, -5, 0])
    if k % 512:
        return np.exp2(np.random.permutation(np.resize(levels, k // 32))).repeat(32)
    a = np.empty((k // 512, 16))
    for p in range(k // 512):
        a[p, :8] = np.random.permutation(np.resize(levels, 8))
        for g in range(8):
            far = levels[np.abs(levels - a[p, g]) >= 10]
            a[p, g + 8] = far[np.random.randint(len(far))]
    return np.exp2(a.ravel()).repeat(32)


BF16 = ml_dtypes.bfloat16


def bf(x):
    return np.asarray(x, np.float32).astype(BF16)


def f64(x):
    return np.asarray(x).astype(np.float64)


B, A, G, H1, H2 = 1024, 128, 5, 2048, 2048
SLOPE = 0.4


def leaky(v):
    return np.where(v >= 0.0, v, SLOPE * v)


def draw0():
    s, t = mx_kscale(H1), mx_kscale(H2)
    keep = np.where(np.random.uniform(size=(B, A)) > 0.2, 1.0, 0.0)
    return {"x": bf(np.random.standard_normal((B, A * G)) * np.repeat(keep, G, axis=1)),
            "h1": bf(leaky(np.random.standard_normal((B, H1))) * s),
            "W2": bf(np.random.standard_normal((H1, H2)) * 1.3 / np.sqrt(H1) / s[:, None] * t),
            "b2": bf(np.random.standard_normal(H2) * 0.3 * t),
            "W3": bf(np.random.standard_normal((H2, A)) * 2.5 / np.sqrt(H2) / t[:, None]),
            "b3": bf(np.random.standard_normal(A) * 0.5)}


def core(x, h1, W2, b2, W3, b3):
    gsum = f64(x).reshape(B, A, G).sum(axis=-1)
    mask = gsum != 0.0
    h2 = leaky((mxq(f64(h1), 1, "e4m3") @ mxq(f64(W2), 0, "e4m3")) + f64(b2))
    logits = (mxq(h2, 1, "e4m3") @ mxq(f64(W3), 0, "e4m3")) + f64(b3)
    logits = np.where(mask, logits, -np.inf)
    e = np.exp(logits - logits.max(axis=1, keepdims=True))
    return e / e.sum(axis=1, keepdims=True)


def e4m3fn_bytes(y):
    return np.clip(np.asarray(y, np.float64), -448.0, 448.0).astype(np.float32).astype(ml_dtypes.float8_e4m3fn).view(np.uint8)


def e4m3fn_values(b):
    return np.asarray(b, np.uint8).view(ml_dtypes.float8_e4m3fn).astype(np.float64)


def setup_inputs():
    d = draw0()
    x0 = np.asarray(d['h1']).astype(np.float64)
    s = (np.max(np.abs(x0), axis=(0,), keepdims=True) / 448.0).astype(np.float32)
    out = {}
    for k, v in d.items():
        if k == 'h1':
            out['h1_bytes'] = e4m3fn_bytes(x0 / s.astype(np.float64))
            out['h1_scale'] = s
        else:
            out[k] = v
    return out


def reference(x, h1_bytes, h1_scale, W2, b2, W3, b3):
    return core(x, e4m3fn_values(h1_bytes) * h1_scale.astype(np.float64), W2, b2, W3, b3)

@@ -1,0 +1,360 @@
+from contextlib import ExitStack
+
+import concourse.mybir as mybir
+from concourse.masks import make_identity
+
+F32 = mybir.dt.float32
+BF16 = mybir.dt.bfloat16
+U32 = mybir.dt.uint32
+U8 = mybir.dt.uint8
+FP8 = mybir.dt.float8_e4m3fn
+X4 = mybir.dt.float8_e4m3fn_x4
+ALU = mybir.AluOpType
+ACT = mybir.ActivationFunctionType
+AX = mybir.AxisListType
+
+P = 128
+B, A, G, H1, H2 = 1024, 128, 5, 2048, 2048
+FLOPS = 2 * B * H1 * H2 + 2 * B * H2 * A
+SLOPE = 0.4
+BIG = 1e30
+RAWBUFS = 7
+
+ON_VECTOR = {"D011", "D100", "D110", "D210", "D220", "D231", "D301", "D311", "D330"}
+ORDER = """
+D000 D001 D011 D010 E00 E01 A0 D020 A1 T0_1 D021 T0_0 B0_1 A2 B0_0 T1_1 D030 T1_0 B1_0 A3 B1_1
+T2_0 D031 T2_1 E02 B2_0 E03 B2_1 T3_0 D101 C0_0 T3_1 C0_1 C0_2 C0_3 A4 B3_0 B3_1 D111 C1_0 T4_1
+D120 C1_1 C1_2 T4_0 C1_3 A5 M000 D121 M001 D130 D100 M002 D131 D110 M003 E10 F000 E11 G0 B4_1
+E12 B4_0 E13 F001 A6 T5_1 F002 M100 B5_1 F003 T5_0 F100 A7 M101 B5_0 D200 T6_0 T6_1 C2_0 B6_0
+C2_1 M102 C2_2 B6_1 C2_3 L000 F101 T7_0 F102 T7_1 L001 B7_0 M103 B7_1 C3_0 D201 C3_1 G1 C3_2
+C3_3 D210 F103 M010 D220 D211 D231 M011 F010 E20 D221 E21 M012 L100 F011 M013 E22 F012 L101 D230
+M110 Q000 M111 F013 D301 F110 E23 M112 D300 L010 M113 F111 L011 F112 M200 F113 D311 D310 D330
+M201 E30 F200 M202 E31 F201 Q001 D320 Q100 M203 L110 F202 M210 L111 F203 D321 M211 Q010 Q101
+Q011 L200 M212 D331 E32 M213 F210 E33 F211 L201 M300 F212 F213 Q110 M301 Q111 F300 L210 W3i M302
+Q200 Q201 Q210 M303 L211 F301 M310 W3q F302 Q211 F303 M311 p0 F310 L300 M312 F311 L301 M313 F312
+Q300 Q301 p1 F313 Z0 b0 L310 L311 Q310 Q311 b1 Z1 l0 m0 l1 e0 m1 o0 e1 o1
+"""
+
+
+def tile_dqn_pa_kernel(tc, x, h1_bytes, h1_scale, W2, b2, W3, b3, out):
+    nc = tc.nc
+    with ExitStack() as ctx:
+        keep = ctx.enter_context(tc.tile_pool(name="keep", bufs=1))
+        rawp = ctx.enter_context(tc.tile_pool(name="rawp", bufs=RAWBUFS))
+        wgp = ctx.enter_context(tc.tile_pool(name="wgp", bufs=6))
+        hrp = ctx.enter_context(tc.tile_pool(name="hrp", bufs=2))
+        hbp = ctx.enter_context(tc.tile_pool(name="hbp", bufs=5))
+        xp = ctx.enter_context(tc.tile_pool(name="xp", bufs=1))
+        hgp = ctx.enter_context(tc.tile_pool(name="hgp", bufs=2))
+        vp = ctx.enter_context(tc.tile_pool(name="vp", bufs=3))
+        h2p = ctx.enter_context(tc.tile_pool(name="h2p", bufs=5))
+        smp = ctx.enter_context(tc.tile_pool(name="smp", bufs=1))
+        mmp = ctx.enter_context(tc.psum_pool(name="mmp", bufs=4))
+        trp = ctx.enter_context(tc.psum_pool(name="trp", bufs=2))
+        axp = ctx.enter_context(tc.psum_pool(name="axp", bufs=2))
+        ctx.enter_context(tc.manual_schedule())
+
+        ident = keep.tile([P, P], F32, name="ident")
+        identb = keep.tile([P, P], BF16, name="identb")
+        h1b = {}
+        sct = keep.tile([P, H1], F32, name="sct", align_bytes=64)
+        h1c = keep.tile([P, 4, B], U32, name="h1c", align_bytes=256)
+        h1s = keep.tile([P, 4, B], U8, name="h1s", align_bytes=256)
+        w2c = keep.tile([P, 4, 4, 512], U32, name="w2c", align_bytes=256)
+        w2s = keep.tile([P, 4, 4, 512], U8, name="w2s", align_bytes=256)
+        h2c = keep.tile([P, 4, B], U32, name="h2c", align_bytes=256)
+        h2s = keep.tile([P, 4, B], U8, name="h2s", align_bytes=256)
+        w3c = keep.tile([P, 4 * A], U32, name="w3c", align_bytes=256)
+        w3s = keep.tile([P, 4 * A], U8, name="w3s", align_bytes=256)
+        b2r = keep.tile([P, P], BF16, name="b2r")
+        b2c = keep.tile([P, 16], F32, name="b2c")
+        b3t = keep.tile([P, A], BF16, name="b3t")
+        pb = keep.tile([P, 8, A], F32, name="pb")
+        dummy = keep.tile([P, 1], F32, name="dummy")
+
+        raw = {}
+        wg = {}
+        hrow = {}
+        tr = {}
+        hg = {}
+        mm = {}
+        v = {}
+        h2b = {}
+        aux = {}
+        sm = {}
+        xts = {}
+        w3 = {}
+
+        def load_x(h):
+            xts[h] = xp.tile([P, 4, A * G], BF16, name="xt", align_bytes=64)
+            nc.sync.dma_start(out=xts[h][:], in_=x[512 * h : 512 * h + 512, :].rearrange("(n p) f -> p n f", p=P))
+
+        def load_w2(g, c):
+            raw[g, c] = rawp.tile([P, 4, 512], BF16, name="raw", align_bytes=64)
+            src = W2[512 * c : 512 * c + 512, 512 * g : 512 * g + 512].rearrange("(p j) n -> p j n", j=4)
+            if (g, c) == (0, 0):
+                nc.sync.dma_start(out=raw[g, c][:, :, 0:256], in_=src[:, :, 0:256])
+                nc.sync.dma_start(out=raw[g, c][:, :, 256:512], in_=src[:, :, 256:512])
+            else:
+                nc.sync.dma_start(out=raw[g, c][:], in_=src)
+
+        def load_h1(b):
+            h1b[b] = hbp.tile([P, H1], U8, name="h1b", align_bytes=64)
+            nc.sync.dma_start(out=h1b[b][:], in_=h1_bytes[P * b : P * b + P, :])
+
+        def op_D(g, c, k):
+            if (g, c) not in wg:
+                wg[g, c] = wgp.tile([P, 2048], BF16, name="wg", align_bytes=256)
+            dst = wg[g, c][:].rearrange("p (t q r j) -> p t q r j", t=4, q=16, r=8)[:, :, 8 * k : 8 * k + 8, :, :]
+            src = raw[g, c][:, :, 256 * k : 256 * k + 256].rearrange("p j (q t r) -> p t q r j", q=8, t=4)
+
+            if "D%d%d%d" % (g, c, k) in ON_VECTOR:
+                nc.vector.tensor_copy(out=dst, in_=src)
+            else:
+                nc.scalar.copy(out=dst, in_=src)
+
+        def op_E(g, c):
+            nc.vector.quantize_mx(out=w2c[:, g, c, :].bitcast(X4), scales=w2s[:, g, c, :], in_=wg[g, c][:])
+
+        def op_A(b):
+            hrow[b] = hrp.tile([P, H1], BF16, name="hrow", align_bytes=64)
+            nc.vector.tensor_tensor(out=hrow[b][:], in0=h1b[b][:].bitcast(FP8), in1=sct[:], op=ALU.mult)
+
+        def op_T(b, i):
+            tr[b, i] = trp.tile([P, 2, 2, P], F32, name="tr")
+            words = hrow[b][:].bitcast(F32)
+            for cc in range(2):
+                for u in range(2):
+                    w0 = 256 * (2 * i + cc) + u
+                    nc.tensor.transpose(tr[b, i][:, cc, u, :], words[:, w0 : 256 * (2 * i + cc + 1) : 2], ident[:])
+
+        def op_B(b, i):
+            q = b // 2
+            if q not in hg:
+                hg[q] = hgp.tile([P, 4, 1024], BF16, name="hg", align_bytes=256)
+            o = (b % 2) * 256
+            dst = hg[q][:].bitcast(F32)[:, 2 * i : 2 * i + 2, o : o + 256].rearrange("p c (r u) -> p c r u", u=2)
+            nc.scalar.copy(out=dst, in_=tr[b, i][:].rearrange("p c u r -> p c r u"))
+
+        def op_C(q, c):
+            nc.vector.quantize_mx(
+                out=h1c[:, c, 256 * q : 256 * q + 256].bitcast(X4),
+                scales=h1s[:, c, 256 * q : 256 * q + 256],
+                in_=hg[q][:, c, :],
+            )
+
+        def op_M(g, h, t):
+            mm[g, h, t] = mmp.tile([P, 512], F32, name="mm")
+            for c in range(4):
+                nc.tensor.matmul_mx(
+                    out=mm[g, h, t][:],
+                    lhsT=w2c[:, g, c, P * t : P * t + P].bitcast(X4),
+                    lhsT_scale=w2s[:, g, c, P * t : P * t + P],
+                    rhs=h1c[:, c, 512 * h : 512 * h + 512].bitcast(X4),
+                    rhs_scale=h1s[:, c, 512 * h : 512 * h + 512],
+                    start=(c == 0),
+                    stop=(c == 3),
+                )
+
+        def op_F(g, h, t):
+            if (g, h) not in v:
+                v[g, h] = vp.tile([P, 4, 512], F32, name="v", align_bytes=64)
+            nc.scalar.activation(
+                out=v[g, h][:, t, :], in_=mm[g, h, t][:], func=ACT.Identity, bias=b2c[:, 4 * g + t : 4 * g + t + 1], scale=1.0
+            )
+
+        def op_L(g, h, k):
+            h2b[g, h, k] = h2p.tile([P, 256, 4], BF16, name="h2b", align_bytes=64)
+            src = v[g, h][:, :, 256 * k : 256 * k + 256].rearrange("p t r -> p r t")
+            nc.vector.scalar_tensor_tensor(
+                out=h2b[g, h, k][:], in0=src, scalar=SLOPE, in1=src, op0=ALU.mult, op1=ALU.max
+            )
+
+        def op_Q(g, h, k):
+            o = 512 * h + 256 * k
+            nc.vector.quantize_mx(
+                out=h2c[:, g, o : o + 256].bitcast(X4),
+                scales=h2s[:, g, o : o + 256],
+                in_=h2b[g, h, k][:].rearrange("p r t -> p (r t)"),
+            )
+
+        def op_G(h):
+            xt = xts[h]
+            aux["g", h] = axp.tile([P, 4, A], F32, name="aux")
+            xv = xt[:].rearrange("p n (a f) -> p n a f", f=G)
+            for f in range(G):
+                nc.tensor.matmul(
+                    aux["g", h][:], lhsT=identb[:], rhs=xv[:, :, :, f], start=(f == 0), stop=(f == G - 1)
+                )
+
+        def op_p(h):
+            nc.vector.tensor_scalar(
+                out=pb[:, 4 * h : 4 * h + 4, :], in0=aux["g", h][:], scalar1=0.0, scalar2=-BIG, op0=ALU.is_equal, op1=ALU.mult
+            )
+
+        def op_b(h):
+            nc.vector.tensor_tensor(
+                out=pb[:, 4 * h : 4 * h + 4, :],
+                in0=pb[:, 4 * h : 4 * h + 4, :],
+                in1=b3t[:].unsqueeze(1).to_broadcast([P, 4, A]),
+                op=ALU.add,
+            )
+
+        def op_Z(h):
+            aux["z", h] = axp.tile([P, 4, A], F32, name="aux")
+            for n in range(4):
+                o = 512 * h + P * n
+                for g in range(4):
+                    nc.tensor.matmul_mx(
+                        out=aux["z", h][:, n, :],
+                        lhsT=h2c[:, g, o : o + P].bitcast(X4),
+                        lhsT_scale=h2s[:, g, o : o + P],
+                        rhs=w3c[:, A * g : A * g + A].bitcast(X4),
+                        rhs_scale=w3s[:, A * g : A * g + A],
+                        start=(g == 0),
+                        stop=(g == 3),
+                    )
+
+        def op_l(h):
+            sm["l", h] = smp.tile([P, 4, A], F32, name="lt%d" % h)
+            nc.vector.tensor_tensor(out=sm["l", h][:], in0=aux["z", h][:], in1=pb[:, 4 * h : 4 * h + 4, :], op=ALU.add)
+
+        def op_m(h):
+            sm["m", h] = smp.tile([P, 4], F32, name="mx%d" % h)
+            sm["n", h] = smp.tile([P, 4], F32, name="ng%d" % h)
+            nc.vector.tensor_reduce(out=sm["m", h][:], in_=sm["l", h][:], axis=AX.X, op=ALU.max)
+            nc.vector.tensor_scalar(out=sm["n", h][:], in0=sm["m", h][:], scalar1=-1.0, scalar2=None, op0=ALU.mult)
+
+        def op_e(h):
+            sm["e", h] = smp.tile([P, 4, A], F32, name="et%d" % h)
+            sm["s", h] = smp.tile([P, 4], F32, name="su%d" % h)
+            for n in range(4):
+                nc.scalar.activation(
+                    out=sm["e", h][:, n, :],
+                    in_=sm["l", h][:, n, :],
+                    func=ACT.Exp,
+                    bias=sm["n", h][:, n : n + 1],
+                    scale=1.0,
+                    accum_out=sm["s", h][:, n : n + 1],
+                )
+
+        def op_o(h):
+            rs = smp.tile([P, 4], F32, name="rs%d" % h)
+            ot = sm["e", h]
+            nc.vector.reciprocal(out=rs[:], in_=sm["s", h][:])
+            for n in range(4):
+                nc.vector.tensor_scalar(
+                    out=ot[:, n, :], in0=sm["e", h][:, n, :], scalar1=rs[:, n : n + 1], scalar2=None, op0=ALU.mult
+                )
+            nc.sync.dma_start(out=out[512 * h : 512 * h + 512, :].rearrange("(n p) a -> p n a", p=P), in_=ot[:])
+
+        def op_W3i():
+            w3["g"] = wgp.tile([P, 2048], BF16, name="wg", align_bytes=256)
+            nc.scalar.copy(
+                out=w3["g"][:].rearrange("p (g a t) -> p g a t", g=4, t=4), in_=w3["r"][:].rearrange("p g (t a) -> p g a t", t=4)
+            )
+
+        def op_W3q():
+            nc.vector.quantize_mx(out=w3c[:].bitcast(X4), scales=w3s[:], in_=w3["g"][:])
+
+        nc.vector.memset(dummy[:], 0.0)
+        nc.scalar.activation(out=dummy[:], in_=dummy[:], func=ACT.Exp)
+        nc.vector.memset(b2r[:], 0.0)
+        units = [(g, c) for g in range(4) for c in range(4)]
+        load_w2(0, 0)
+        load_w2(0, 1)
+        nc.sync.dma_start(out=sct[:], in_=h1_scale.rearrange("o k -> (o k)").partition_broadcast(P))
+        load_h1(0)
+        load_w2(0, 2)
+        load_h1(1)
+        load_h1(2)
+        load_w2(0, 3)
+        load_h1(3)
+        for g in range(4):
+            nc.sync.dma_start(
+                out=b2r[4 * g : 4 * g + 4, :].rearrange("t (q r) -> t q r", q=16),
+                in_=b2[512 * g : 512 * g + 512].rearrange("(q t r) -> t q r", q=16, t=4),
+            )
+        load_w2(1, 0)
+        load_h1(4)
+        load_w2(1, 1)
+        load_w2(1, 2)
+        make_identity(nc, ident[:])
+        make_identity(nc, identb[:])
+        nc.sync.dma_start(out=b3t[:], in_=b3.partition_broadcast(P))
+
+        def load_w3():
+            w3["r"] = rawp.tile([P, 4, 512], BF16, name="raw", align_bytes=64)
+            for g in range(4):
+                for t in range(4):
+                    nc.sync.dma_start(
+                        out=w3["r"][:, g, A * t : A * t + A],
+                        in_=W3[512 * g : 512 * g + 512, :].rearrange("(q t r) a -> t q r a", q=16, t=4)[t],
+                    )
+
+        nxt = RAWBUFS
+        seen = {}
+        for name in ORDER.split():
+            if name in ("W3i", "W3q"):
+                if name == "W3i":
+                    op_W3i()
+                else:
+                    op_W3q()
+                continue
+            kind = name[0]
+            rest = name[1:].replace("_", "")
+            args = [int(ch) for ch in rest]
+            if kind == "F" and "b2" not in seen:
+                seen["b2"] = 1
+            if kind == "D":
+                op_D(*args)
+                key = (args[0], args[1])
+                seen[key] = seen.get(key, 0) + 1
+                while nxt < 17 and seen.get(divmod(nxt - RAWBUFS, 4), 0) == 2:
+                    if nxt < 16:
+                        load_w2(*units[nxt])
+                    else:
+                        load_w3()
+                    if nxt in (9, 11):
+                        load_x((nxt - 9) // 2)
+                    nxt += 1
+            elif kind == "A":
+                op_A(*args)
+                if args[0] < 3:
+                    load_h1(args[0] + 5)
+            elif kind == "T":
+                op_T(*args)
+                if args == [1, 1]:
+                    bp = axp.tile([P, P], BF16, name="aux")
+                    nc.tensor.transpose(bp[:], b2r[:], identb[:])
+                    nc.vector.tensor_copy(out=b2c[:], in_=bp[:, 0:16])
+            elif kind == "B":
+                op_B(*args)
+            elif kind == "C":
+                op_C(*args)
+            elif kind == "E":
+                op_E(*args)
+            elif kind == "M":
+                op_M(*args)
+            elif kind == "F":
+                op_F(*args)
+            elif kind == "L":
+                op_L(*args)
+            elif kind == "Q":
+                op_Q(*args)
+            elif kind == "G":
+                op_G(*args)
+            elif kind == "p":
+                op_p(*args)
+            elif kind == "b":
+                op_b(*args)
+            elif kind == "Z":
+                op_Z(*args)
+            elif kind == "l":
+                op_l(*args)
+            elif kind == "m":
+                op_m(*args)
+            elif kind == "e":
+                op_e(*args)
+            elif kind == "o":
+                op_o(*args)

@@ -20,19 +20,21 @@ SLOPE = 0.4
 BIG = 1e30
 RAWBUFS = 7
 
-ON_VECTOR = {"D011", "D100", "D110", "D210", "D220", "D231", "D301", "D311", "D330"}
+ON_VECTOR = {"D001", "D011", "D120", "D121", "D131", "D201", "D230", "D331"}
 ORDER = """
-D000 D001 D011 D010 E00 E01 A0 D020 A1 T0_1 D021 T0_0 B0_1 A2 B0_0 T1_1 D030 T1_0 B1_0 A3 B1_1
-T2_0 D031 T2_1 E02 B2_0 E03 B2_1 T3_0 D101 C0_0 T3_1 C0_1 C0_2 C0_3 A4 B3_0 B3_1 D111 C1_0 T4_1
-D120 C1_1 C1_2 T4_0 C1_3 A5 M000 D121 M001 D130 D100 M002 D131 D110 M003 E10 F000 E11 G0 B4_1
-E12 B4_0 E13 F001 A6 T5_1 F002 M100 B5_1 F003 T5_0 F100 A7 M101 B5_0 D200 T6_0 T6_1 C2_0 B6_0
-C2_1 M102 C2_2 B6_1 C2_3 L000 F101 T7_0 F102 T7_1 L001 B7_0 M103 B7_1 C3_0 D201 C3_1 G1 C3_2
-C3_3 D210 F103 M010 D220 D211 D231 M011 F010 E20 D221 E21 M012 L100 F011 M013 E22 F012 L101 D230
-M110 Q000 M111 F013 D301 F110 E23 M112 D300 L010 M113 F111 L011 F112 M200 F113 D311 D310 D330
-M201 E30 F200 M202 E31 F201 Q001 D320 Q100 M203 L110 F202 M210 L111 F203 D321 M211 Q010 Q101
-Q011 L200 M212 D331 E32 M213 F210 E33 F211 L201 M300 F212 F213 Q110 M301 Q111 F300 L210 W3i M302
-Q200 Q201 Q210 M303 L211 F301 M310 W3q F302 Q211 F303 M311 p0 F310 L300 M312 F311 L301 M313 F312
-Q300 Q301 p1 F313 Z0 b0 L310 L311 Q310 Q311 b1 Z1 l0 m0 l1 e0 m1 o0 e1 o1
+D000 D001 E00 D010 D011 E01 A0_0 T0_0 A0_1 B0_0 A1 T0_1 D020 B0_1 A2 T1_1 D021 T1_0 B1_0 A3 B1_1
+D030 T2_1 T2_0 B2_1 C0_0 C0_1 B2_0 C0_2 T3_1 C0_3 D031 A4 T3_0 G0 B3_0 B3_1 C1_0 D100 C1_1 T4_1
+C1_2 C1_3 A5 T4_0 D101 G1 B4_0 B4_1 E02 D110 T5_1 E03 T5_0 A6 B5_1 M0010 B5_0 M0011 F0010 D111
+M0012 C2_0 T6_0 C2_1 C2_2 F0011 C2_3 T6_1 B6_0 A7 M0013 F0012 B6_1 M0110 F0013 M0111 D130 M0112
+D120 T7_0 D121 F0110 F0111 T7_1 D131 B7_0 M0113 F0112 E10 B7_1 C3_0 F0113 C3_1 D200 C3_2 C3_3
+E11 M0220 D210 E12 E13 M0221 D201 F0220 D211 M0222 D230 L00 M0223 F0221 F0222 L01 M1020 D220
+M1021 E20 F0223 E21 F1020 M1022 L02 F1021 D221 M1023 L03 F1022 M1220 F1023 E22 D231 M1221 Q00
+D331 M1222 F1220 L10 F1221 M1223 D300 E23 L11 M2020 F1222 F1223 M2021 Q01 F2020 Q02 Q03 D301 Q10
+M2022 L12 F2021 M2023 F2022 E30 D310 L13 M2220 M2221 F2023 Q11 p0 D311 M2222 L20 D320 M2223 E31
+L21 D321 D330 p1 E32 F2220 Q12 E33 F2221 Q13 M3020 F2222 Q20 Q21 F2223 b0 M3021 W3i b1 L22 M3022
+L23 M3023 F3020 F3021 M3210 Q22 F3022 Q23 M3211 W3q F3023 M3212 F3210 L30 M3213 F3211 F3212
+M3310 F3213 M3311 L31 F3310 M3312 F3311 M3313 F3312 Q30 Q31 F3313 Z0 L32 Z1 l0 l1 Q32 L33 Z2 l2
+Q33 m0 Z3 m1 e0 m2 e1 l3 e2 r0 r1 o0 m3 o1 r2 e3 o2 r3 o3
 """
 
 
@@ -43,8 +45,8 @@ def tile_dqn_pa_kernel(tc, x, h1_bytes, h1_scale, W2, b2, W3, b3, out):
         rawp = ctx.enter_context(tc.tile_pool(name="rawp", bufs=RAWBUFS))
         wgp = ctx.enter_context(tc.tile_pool(name="wgp", bufs=6))
         hrp = ctx.enter_context(tc.tile_pool(name="hrp", bufs=2))
-        hbp = ctx.enter_context(tc.tile_pool(name="hbp", bufs=5))
-        xp = ctx.enter_context(tc.tile_pool(name="xp", bufs=1))
+        hbp = ctx.enter_context(tc.tile_pool(name="hbp", bufs=6))
+        xp = ctx.enter_context(tc.tile_pool(name="xp", bufs=2))
         hgp = ctx.enter_context(tc.tile_pool(name="hgp", bufs=2))
         vp = ctx.enter_context(tc.tile_pool(name="vp", bufs=3))
         h2p = ctx.enter_context(tc.tile_pool(name="h2p", bufs=5))
@@ -89,12 +91,13 @@ def tile_dqn_pa_kernel(tc, x, h1_bytes, h1_scale, W2, b2, W3, b3, out):
             xts[h] = xp.tile([P, 4, A * G], BF16, name="xt", align_bytes=64)
             nc.sync.dma_start(out=xts[h][:], in_=x[512 * h : 512 * h + 512, :].rearrange("(n p) f -> p n f", p=P))
 
-        def load_w2(g, c):
-            raw[g, c] = rawp.tile([P, 4, 512], BF16, name="raw", align_bytes=64)
+        def load_w2(g, c, part=None):
+            if part in (None, 0):
+                raw[g, c] = rawp.tile([P, 4, 512], BF16, name="raw", align_bytes=64)
             src = W2[512 * c : 512 * c + 512, 512 * g : 512 * g + 512].rearrange("(p j) n -> p j n", j=4)
-            if (g, c) == (0, 0):
-                nc.sync.dma_start(out=raw[g, c][:, :, 0:256], in_=src[:, :, 0:256])
-                nc.sync.dma_start(out=raw[g, c][:, :, 256:512], in_=src[:, :, 256:512])
+            if part is not None:
+                cols = slice(256 * part, 256 * part + 256)
+                nc.sync.dma_start(out=raw[g, c][:, :, cols], in_=src[:, :, cols])
             else:
                 nc.sync.dma_start(out=raw[g, c][:], in_=src)
 
@@ -108,17 +111,43 @@ def tile_dqn_pa_kernel(tc, x, h1_bytes, h1_scale, W2, b2, W3, b3, out):
             dst = wg[g, c][:].rearrange("p (t q r j) -> p t q r j", t=4, q=16, r=8)[:, :, 8 * k : 8 * k + 8, :, :]
             src = raw[g, c][:, :, 256 * k : 256 * k + 256].rearrange("p j (q t r) -> p t q r j", q=8, t=4)
 
+            dst = dst.rearrange("p t q r j -> p t q j r")
+            src = src.rearrange("p t q r j -> p t q j r")
             if "D%d%d%d" % (g, c, k) in ON_VECTOR:
                 nc.vector.tensor_copy(out=dst, in_=src)
             else:
                 nc.scalar.copy(out=dst, in_=src)
 
+        def op_I(g, c, k):
+            tr["I", g, c, k] = trp.tile([P, 1024], BF16, name="tr")
+            dst = tr["I", g, c, k][:].rearrange("p (n j) -> p j n", j=4)
+            src = raw[g, c][:].rearrange("p j (q t r) -> p j t q r", q=16, t=4)
+            for j in range(4):
+                nc.tensor.matmul(
+                    dst[:, j, :].rearrange("p (t q r) -> p t q r", t=2, q=16),
+                    lhsT=identb[:],
+                    rhs=src[:, j, 2 * k : 2 * k + 2, :, :],
+                    start=True,
+                    stop=True,
+                )
+
+        def op_K(g, c, k):
+            if (g, c) not in wg:
+                wg[g, c] = wgp.tile([P, 2048], BF16, name="wg", align_bytes=256)
+            dst = wg[g, c][:, 1024 * k : 1024 * k + 1024]
+            if "D%d%d%d" % (g, c, k) in ON_VECTOR:
+                nc.vector.tensor_copy(out=dst, in_=tr["I", g, c, k][:])
+            else:
+                nc.scalar.copy(out=dst, in_=tr["I", g, c, k][:])
+
         def op_E(g, c):
             nc.vector.quantize_mx(out=w2c[:, g, c, :].bitcast(X4), scales=w2s[:, g, c, :], in_=wg[g, c][:])
 
-        def op_A(b):
-            hrow[b] = hrp.tile([P, H1], BF16, name="hrow", align_bytes=64)
-            nc.vector.tensor_tensor(out=hrow[b][:], in0=h1b[b][:].bitcast(FP8), in1=sct[:], op=ALU.mult)
+        def op_A(b, i=None):
+            if b not in hrow:
+                hrow[b] = hrp.tile([P, H1], BF16, name="hrow", align_bytes=64)
+            sl = slice(0, H1) if i is None else slice(1024 * i, 1024 * i + 1024)
+            nc.vector.tensor_tensor(out=hrow[b][:, sl], in0=h1b[b][:, sl].bitcast(FP8), in1=sct[:, sl], op=ALU.mult)
 
         def op_T(b, i):
             tr[b, i] = trp.tile([P, 2, 2, P], F32, name="tr")
@@ -143,39 +172,44 @@ def tile_dqn_pa_kernel(tc, x, h1_bytes, h1_scale, W2, b2, W3, b3, out):
                 in_=hg[q][:, c, :],
             )
 
-        def op_M(g, h, t):
-            mm[g, h, t] = mmp.tile([P, 512], F32, name="mm")
+        def op_M(g, q, n, t):
+            mm[g, q, t] = mmp.tile([P, 512], F32, name="mm")
+            cols = slice(256 * q, 256 * (q + n))
             for c in range(4):
                 nc.tensor.matmul_mx(
-                    out=mm[g, h, t][:],
+                    out=mm[g, q, t][:, 0 : 256 * n],
                     lhsT=w2c[:, g, c, P * t : P * t + P].bitcast(X4),
                     lhsT_scale=w2s[:, g, c, P * t : P * t + P],
-                    rhs=h1c[:, c, 512 * h : 512 * h + 512].bitcast(X4),
-                    rhs_scale=h1s[:, c, 512 * h : 512 * h + 512],
+                    rhs=h1c[:, c, cols].bitcast(X4),
+                    rhs_scale=h1s[:, c, cols],
                     start=(c == 0),
                     stop=(c == 3),
                 )
 
-        def op_F(g, h, t):
+        def op_F(g, q, n, t):
+            h = q // 2
             if (g, h) not in v:
                 v[g, h] = vp.tile([P, 4, 512], F32, name="v", align_bytes=64)
+            o = 256 * (q - 2 * h)
             nc.scalar.activation(
-                out=v[g, h][:, t, :], in_=mm[g, h, t][:], func=ACT.Identity, bias=b2c[:, 4 * g + t : 4 * g + t + 1], scale=1.0
+                out=v[g, h][:, t, o : o + 256 * n],
+                in_=mm[g, q, t][:, 0 : 256 * n],
+                func=ACT.Identity,
+                bias=b2c[:, 4 * g + t : 4 * g + t + 1],
+                scale=1.0,
             )
 
-        def op_L(g, h, k):
-            h2b[g, h, k] = h2p.tile([P, 256, 4], BF16, name="h2b", align_bytes=64)
-            src = v[g, h][:, :, 256 * k : 256 * k + 256].rearrange("p t r -> p r t")
-            nc.vector.scalar_tensor_tensor(
-                out=h2b[g, h, k][:], in0=src, scalar=SLOPE, in1=src, op0=ALU.mult, op1=ALU.max
-            )
+        def op_L(g, q):
+            h2b[g, q] = h2p.tile([P, 256, 4], BF16, name="h2b", align_bytes=64)
+            o = 256 * (q % 2)
+            src = v[g, q // 2][:, :, o : o + 256].rearrange("p t r -> p r t")
+            nc.vector.scalar_tensor_tensor(out=h2b[g, q][:], in0=src, scalar=SLOPE, in1=src, op0=ALU.mult, op1=ALU.max)
 
-        def op_Q(g, h, k):
-            o = 512 * h + 256 * k
+        def op_Q(g, q):
             nc.vector.quantize_mx(
-                out=h2c[:, g, o : o + 256].bitcast(X4),
-                scales=h2s[:, g, o : o + 256],
-                in_=h2b[g, h, k][:].rearrange("p r t -> p (r t)"),
+                out=h2c[:, g, 256 * q : 256 * q + 256].bitcast(X4),
+                scales=h2s[:, g, 256 * q : 256 * q + 256],
+                in_=h2b[g, q][:].rearrange("p r t -> p (r t)"),
             )
 
         def op_G(h):
@@ -200,13 +234,13 @@ def tile_dqn_pa_kernel(tc, x, h1_bytes, h1_scale, W2, b2, W3, b3, out):
                 op=ALU.add,
             )
 
-        def op_Z(h):
-            aux["z", h] = axp.tile([P, 4, A], F32, name="aux")
-            for n in range(4):
-                o = 512 * h + P * n
+        def op_Z(q):
+            aux["z", q] = axp.tile([P, 2, A], F32, name="aux")
+            for n in range(2):
+                o = 256 * q + P * n
                 for g in range(4):
                     nc.tensor.matmul_mx(
-                        out=aux["z", h][:, n, :],
+                        out=aux["z", q][:, n, :],
                         lhsT=h2c[:, g, o : o + P].bitcast(X4),
                         lhsT_scale=h2s[:, g, o : o + P],
                         rhs=w3c[:, A * g : A * g + A].bitcast(X4),
@@ -215,38 +249,40 @@ def tile_dqn_pa_kernel(tc, x, h1_bytes, h1_scale, W2, b2, W3, b3, out):
                         stop=(g == 3),
                     )
 
-        def op_l(h):
-            sm["l", h] = smp.tile([P, 4, A], F32, name="lt%d" % h)
-            nc.vector.tensor_tensor(out=sm["l", h][:], in0=aux["z", h][:], in1=pb[:, 4 * h : 4 * h + 4, :], op=ALU.add)
+        def op_l(q):
+            sm["l", q] = smp.tile([P, 2, A], F32, name="lt%d" % q)
+            nc.vector.tensor_tensor(out=sm["l", q][:], in0=aux["z", q][:], in1=pb[:, 2 * q : 2 * q + 2, :], op=ALU.add)
 
-        def op_m(h):
-            sm["m", h] = smp.tile([P, 4], F32, name="mx%d" % h)
-            sm["n", h] = smp.tile([P, 4], F32, name="ng%d" % h)
-            nc.vector.tensor_reduce(out=sm["m", h][:], in_=sm["l", h][:], axis=AX.X, op=ALU.max)
-            nc.vector.tensor_scalar(out=sm["n", h][:], in0=sm["m", h][:], scalar1=-1.0, scalar2=None, op0=ALU.mult)
+        def op_m(q):
+            sm["m", q] = smp.tile([P, 2], F32, name="mx%d" % q)
+            sm["n", q] = smp.tile([P, 2], F32, name="ng%d" % q)
+            nc.vector.tensor_reduce(out=sm["m", q][:], in_=sm["l", q][:], axis=AX.X, op=ALU.max)
+            nc.vector.tensor_scalar(out=sm["n", q][:], in0=sm["m", q][:], scalar1=-1.0, scalar2=None, op0=ALU.mult)
 
-        def op_e(h):
-            sm["e", h] = smp.tile([P, 4, A], F32, name="et%d" % h)
-            sm["s", h] = smp.tile([P, 4], F32, name="su%d" % h)
-            for n in range(4):
+        def op_e(q):
+            sm["e", q] = smp.tile([P, 2, A], F32, name="et%d" % q)
+            sm["s", q] = smp.tile([P, 2], F32, name="su%d" % q)
+            for n in range(2):
                 nc.scalar.activation(
-                    out=sm["e", h][:, n, :],
-                    in_=sm["l", h][:, n, :],
+                    out=sm["e", q][:, n, :],
+                    in_=sm["l", q][:, n, :],
                     func=ACT.Exp,
-                    bias=sm["n", h][:, n : n + 1],
+                    bias=sm["n", q][:, n : n + 1],
                     scale=1.0,
-                    accum_out=sm["s", h][:, n : n + 1],
+                    accum_out=sm["s", q][:, n : n + 1],
                 )
 
-        def op_o(h):
-            rs = smp.tile([P, 4], F32, name="rs%d" % h)
-            ot = sm["e", h]
-            nc.vector.reciprocal(out=rs[:], in_=sm["s", h][:])
-            for n in range(4):
-                nc.vector.tensor_scalar(
-                    out=ot[:, n, :], in0=sm["e", h][:, n, :], scalar1=rs[:, n : n + 1], scalar2=None, op0=ALU.mult
+        def op_r(q):
+            sm["r", q] = smp.tile([P, 2], F32, name="rs%d" % q)
+            nc.vector.reciprocal(out=sm["r", q][:], in_=sm["s", q][:])
+
+        def op_o(q):
+            ot = sm["l", q]
+            for n in range(2):
+                nc.scalar.activation(
+                    out=ot[:, n, :], in_=sm["e", q][:, n, :], func=ACT.Copy, scale=sm["r", q][:, n : n + 1]
                 )
-            nc.sync.dma_start(out=out[512 * h : 512 * h + 512, :].rearrange("(n p) a -> p n a", p=P), in_=ot[:])
+            nc.sync.dma_start(out=out[256 * q : 256 * q + 256, :].rearrange("(n p) a -> p n a", p=P), in_=ot[:])
 
         def op_W3i():
             w3["g"] = wgp.tile([P, 2048], BF16, name="wg", align_bytes=256)
@@ -261,27 +297,35 @@ def tile_dqn_pa_kernel(tc, x, h1_bytes, h1_scale, W2, b2, W3, b3, out):
         nc.scalar.activation(out=dummy[:], in_=dummy[:], func=ACT.Exp)
         nc.vector.memset(b2r[:], 0.0)
         units = [(g, c) for g in range(4) for c in range(4)]
-        load_w2(0, 0)
-        load_w2(0, 1)
-        nc.sync.dma_start(out=sct[:], in_=h1_scale.rearrange("o k -> (o k)").partition_broadcast(P))
-        load_h1(0)
-        load_w2(0, 2)
-        load_h1(1)
-        load_h1(2)
-        load_w2(0, 3)
-        load_h1(3)
-        for g in range(4):
+
+        def load_sc(i):
             nc.sync.dma_start(
-                out=b2r[4 * g : 4 * g + 4, :].rearrange("t (q r) -> t q r", q=16),
-                in_=b2[512 * g : 512 * g + 512].rearrange("(q t r) -> t q r", q=16, t=4),
+                out=sct[:, 1024 * i : 1024 * i + 1024],
+                in_=h1_scale.rearrange("o k -> (o k)")[1024 * i : 1024 * i + 1024].partition_broadcast(P),
             )
-        load_w2(1, 0)
-        load_h1(4)
-        load_w2(1, 1)
-        load_w2(1, 2)
+
+        def load_b2():
+            for g in range(4):
+                nc.sync.dma_start(
+                    out=b2r[4 * g : 4 * g + 4, :].rearrange("t (q r) -> t q r", q=16),
+                    in_=b2[512 * g : 512 * g + 512].rearrange("(q t r) -> t q r", q=16, t=4),
+                )
+
         make_identity(nc, ident[:])
         make_identity(nc, identb[:])
-        nc.sync.dma_start(out=b3t[:], in_=b3.partition_broadcast(P))
+        for name in "W000 W001 W01 S0 H0 S1 H1 W02 H2 b2 W03 H3 W10 H4 X0 X1 W11 H5 W12 b3".split():
+            if name[0] == "W":
+                load_w2(int(name[1]), int(name[2]), int(name[3]) if len(name) > 3 else None)
+            elif name[0] == "S":
+                load_sc(int(name[1]))
+            elif name[0] == "H":
+                load_h1(int(name[1]))
+            elif name[0] == "X":
+                load_x(int(name[1]))
+            elif name == "b2":
+                load_b2()
+            elif name == "b3":
+                nc.sync.dma_start(out=b3t[:], in_=b3.partition_broadcast(P))
 
         def load_w3():
             w3["r"] = rawp.tile([P, 4, 512], BF16, name="raw", align_bytes=64)
@@ -306,8 +350,8 @@ def tile_dqn_pa_kernel(tc, x, h1_bytes, h1_scale, W2, b2, W3, b3, out):
             args = [int(ch) for ch in rest]
             if kind == "F" and "b2" not in seen:
                 seen["b2"] = 1
-            if kind == "D":
-                op_D(*args)
+            if kind in "DI":
+                (op_D if kind == "D" else op_I)(*args)
                 key = (args[0], args[1])
                 seen[key] = seen.get(key, 0) + 1
                 while nxt < 17 and seen.get(divmod(nxt - RAWBUFS, 4), 0) == 2:
@@ -315,21 +359,23 @@ def tile_dqn_pa_kernel(tc, x, h1_bytes, h1_scale, W2, b2, W3, b3, out):
                         load_w2(*units[nxt])
                     else:
                         load_w3()
-                    if nxt in (9, 11):
-                        load_x((nxt - 9) // 2)
                     nxt += 1
+            elif kind == "K":
+                op_K(*args)
             elif kind == "A":
                 op_A(*args)
-                if args[0] < 3:
-                    load_h1(args[0] + 5)
+                seen["A", args[0]] = seen.get(("A", args[0]), 0) + (3 - len(args))
+                if args[0] < 2 and seen["A", args[0]] == 2:
+                    load_h1(args[0] + 6)
             elif kind == "T":
                 op_T(*args)
-                if args == [1, 1]:
+                if args == [1, 0]:
                     bp = axp.tile([P, P], BF16, name="aux")
                     nc.tensor.transpose(bp[:], b2r[:], identb[:])
-                    nc.vector.tensor_copy(out=b2c[:], in_=bp[:, 0:16])
             elif kind == "B":
                 op_B(*args)
+                if args == [1, 1]:
+                    nc.scalar.copy(out=b2c[:], in_=bp[:, 0:16])
             elif kind == "C":
                 op_C(*args)
             elif kind == "E":
@@ -356,5 +402,7 @@ def tile_dqn_pa_kernel(tc, x, h1_bytes, h1_scale, W2, b2, W3, b3, out):
                 op_m(*args)
             elif kind == "e":
                 op_e(*args)
+            elif kind == "r":
+                op_r(*args)
             elif kind == "o":
                 op_o(*args)

@@ -20,21 +20,21 @@ SLOPE = 0.4
 BIG = 1e30
 RAWBUFS = 7
 
-ON_VECTOR = {"D001", "D011", "D120", "D121", "D131", "D201", "D230", "D331"}
+ON_VECTOR = {"D000", "D010", "D111", "D120", "D130", "D231", "D300", "D330", "D331"}
 ORDER = """
-D000 D001 E00 D010 D011 E01 A0_0 T0_0 A0_1 B0_0 A1 T0_1 D020 B0_1 A2 T1_1 D021 T1_0 B1_0 A3 B1_1
-D030 T2_1 T2_0 B2_1 C0_0 C0_1 B2_0 C0_2 T3_1 C0_3 D031 A4 T3_0 G0 B3_0 B3_1 C1_0 D100 C1_1 T4_1
-C1_2 C1_3 A5 T4_0 D101 G1 B4_0 B4_1 E02 D110 T5_1 E03 T5_0 A6 B5_1 M0010 B5_0 M0011 F0010 D111
-M0012 C2_0 T6_0 C2_1 C2_2 F0011 C2_3 T6_1 B6_0 A7 M0013 F0012 B6_1 M0110 F0013 M0111 D130 M0112
-D120 T7_0 D121 F0110 F0111 T7_1 D131 B7_0 M0113 F0112 E10 B7_1 C3_0 F0113 C3_1 D200 C3_2 C3_3
-E11 M0220 D210 E12 E13 M0221 D201 F0220 D211 M0222 D230 L00 M0223 F0221 F0222 L01 M1020 D220
-M1021 E20 F0223 E21 F1020 M1022 L02 F1021 D221 M1023 L03 F1022 M1220 F1023 E22 D231 M1221 Q00
-D331 M1222 F1220 L10 F1221 M1223 D300 E23 L11 M2020 F1222 F1223 M2021 Q01 F2020 Q02 Q03 D301 Q10
-M2022 L12 F2021 M2023 F2022 E30 D310 L13 M2220 M2221 F2023 Q11 p0 D311 M2222 L20 D320 M2223 E31
-L21 D321 D330 p1 E32 F2220 Q12 E33 F2221 Q13 M3020 F2222 Q20 Q21 F2223 b0 M3021 W3i b1 L22 M3022
-L23 M3023 F3020 F3021 M3210 Q22 F3022 Q23 M3211 W3q F3023 M3212 F3210 L30 M3213 F3211 F3212
-M3310 F3213 M3311 L31 F3310 M3312 F3311 M3313 F3312 Q30 Q31 F3313 Z0 L32 Z1 l0 l1 Q32 L33 Z2 l2
-Q33 m0 Z3 m1 e0 m2 e1 l3 e2 r0 r1 o0 m3 o1 r2 e3 o2 r3 o3
+D000 D001 D011 D010 E00 E01 A0_0 T0_0 A0_1 B0_0 A1 T0_1 D020 B0_1 A2 T1_1 D021 T1_0 B1_0 A3 B1_1
+D030 T2_1 T2_0 B2_1 C0_0 C0_1 B2_0 C0_2 T3_1 C0_3 D031 E02 T3_0 A4 G0 B3_0 B3_1 D100 G1 C1_0
+C1_1 C1_2 D101 C1_3 E03 A5 D110 T4_1 T4_0 B4_1 M0010 B4_0 M0011 A6 F0010 T5_1 D121 T5_0 M0012
+B5_1 A7 M0013 B5_0 T6_0 F0011 F0012 F0013 T6_1 B6_0 C2_0 M0110 B6_1 C2_1 T7_0 C2_2 D131 C2_3
+D111 T7_1 D120 M0111 B7_0 M0112 D130 B7_1 M0113 F0110 C3_0 F0111 C3_1 F0112 C3_2 F0113 C3_3 D200
+E10 M0220 E11 D201 E12 M0221 E13 D231 M0222 F0220 F0221 L00 M0223 D210 L01 M1020 F0222 F0223 E20
+M1021 F1020 Q00 L02 D211 M1022 L03 F1021 M1023 F1022 E21 D220 M1220 D300 D330 D221 M1221 D331
+M1222 D230 Q01 E22 Q02 F1023 E33 F1220 E23 M1223 F1221 L10 F1222 M2020 F1223 L11 D301 M2021 Q03
+Q10 M2022 F2020 E30 F2021 L12 M2023 D310 L13 M2220 F2022 D311 Q11 M2221 Q12 Q13 p0 D320 M2222
+E31 p1 D321 b0 b1 F2023 E32 F2220 M2223 L20 F2221 F2222 M3020 L21 F2223 W3i M3021 Q20 Q21 L22
+M3022 M3023 L23 F3020 F3021 M3210 F3022 Q22 Q23 M3211 F3023 W3q M3212 F3210 L30 F3211 M3213
+F3212 M3310 F3213 L31 M3311 F3310 M3312 F3311 Q30 M3313 Q31 F3312 L32 Z0 F3313 Z1 l0 Q32 l1 Z2
+L33 l2 Q33 m0 Z3 m1 e0 m2 e1 l3 e2 r0 r1 o0 m3 o1 r2 e3 o2 r3 o3
 """
 
 
@@ -103,7 +103,9 @@ def tile_dqn_pa_kernel(tc, x, h1_bytes, h1_scale, W2, b2, W3, b3, out):
 
         def load_h1(b):
             h1b[b] = hbp.tile([P, H1], U8, name="h1b", align_bytes=64)
-            nc.sync.dma_start(out=h1b[b][:], in_=h1_bytes[P * b : P * b + P, :])
+            q = b // 2
+            rows = h1_bytes[256 * q : 256 * q + 256, :].rearrange("(y j s) k -> j s y k", y=4, j=2)
+            nc.sync.dma_start(out=h1b[b][:], in_=rows[b % 2])
 
         def op_D(g, c, k):
             if (g, c) not in wg:
@@ -189,27 +191,28 @@ def tile_dqn_pa_kernel(tc, x, h1_bytes, h1_scale, W2, b2, W3, b3, out):
         def op_F(g, q, n, t):
             h = q // 2
             if (g, h) not in v:
-                v[g, h] = vp.tile([P, 4, 512], F32, name="v", align_bytes=64)
-            o = 256 * (q - 2 * h)
+                v[g, h] = vp.tile([P, 2, 64, 4, 4], F32, name="v", align_bytes=64)
+            k = q - 2 * h
             nc.scalar.activation(
-                out=v[g, h][:, t, o : o + 256 * n],
-                in_=mm[g, q, t][:, 0 : 256 * n],
+                out=v[g, h][:, k : k + n, :, t, :].rearrange("p k s y -> p (k s) y"),
+                in_=mm[g, q, t][:, 0 : 256 * n].rearrange("p (s y) -> p s y", y=4),
                 func=ACT.Identity,
                 bias=b2c[:, 4 * g + t : 4 * g + t + 1],
                 scale=1.0,
             )
 
         def op_L(g, q):
-            h2b[g, q] = h2p.tile([P, 256, 4], BF16, name="h2b", align_bytes=64)
-            o = 256 * (q % 2)
-            src = v[g, q // 2][:, :, o : o + 256].rearrange("p t r -> p r t")
-            nc.vector.scalar_tensor_tensor(out=h2b[g, q][:], in0=src, scalar=SLOPE, in1=src, op0=ALU.mult, op1=ALU.max)
+            h2b[g, q] = h2p.tile([P, 4, 64, 4], BF16, name="h2b", align_bytes=64)
+            src = v[g, q // 2][:, q % 2, :, :, :].rearrange("p s t y -> p (s t) y")
+            nc.vector.scalar_tensor_tensor(
+                out=h2b[g, q][:].rearrange("p y s t -> p (s t) y"), in0=src, scalar=SLOPE, in1=src, op0=ALU.mult, op1=ALU.max
+            )
 
         def op_Q(g, q):
             nc.vector.quantize_mx(
                 out=h2c[:, g, 256 * q : 256 * q + 256].bitcast(X4),
                 scales=h2s[:, g, 256 * q : 256 * q + 256],
-                in_=h2b[g, q][:].rearrange("p r t -> p (r t)"),
+                in_=h2b[g, q][:].rearrange("p y s t -> p (y s t)"),
             )
 
         def op_G(h):

from contextlib import ExitStack

import concourse.mybir as mybir
from concourse.masks import make_identity

F32 = mybir.dt.float32
BF16 = mybir.dt.bfloat16
U32 = mybir.dt.uint32
U8 = mybir.dt.uint8
FP8 = mybir.dt.float8_e4m3fn
X4 = mybir.dt.float8_e4m3fn_x4
ALU = mybir.AluOpType
ACT = mybir.ActivationFunctionType
AX = mybir.AxisListType

P = 128
B, A, G, H1, H2 = 1024, 128, 5, 2048, 2048
FLOPS = 2 * B * H1 * H2 + 2 * B * H2 * A
SLOPE = 0.4
BIG = 1e30
RAWBUFS = 7

ON_VECTOR = {"D000", "D010", "D111", "D120", "D130", "D231", "D300", "D330", "D331"}
ORDER = """
D000 D001 D011 D010 E00 E01 A0_0 T0_0 A0_1 B0_0 A1 T0_1 D020 B0_1 A2 T1_1 D021 T1_0 B1_0 A3 B1_1
D030 T2_1 T2_0 B2_1 C0_0 C0_1 B2_0 C0_2 T3_1 C0_3 D031 E02 T3_0 A4 G0 B3_0 B3_1 D100 G1 C1_0
C1_1 C1_2 D101 C1_3 E03 A5 D110 T4_1 T4_0 B4_1 M0010 B4_0 M0011 A6 F0010 T5_1 D121 T5_0 M0012
B5_1 A7 M0013 B5_0 T6_0 F0011 F0012 F0013 T6_1 B6_0 C2_0 M0110 B6_1 C2_1 T7_0 C2_2 D131 C2_3
D111 T7_1 D120 M0111 B7_0 M0112 D130 B7_1 M0113 F0110 C3_0 F0111 C3_1 F0112 C3_2 F0113 C3_3 D200
E10 M0220 E11 D201 E12 M0221 E13 D231 M0222 F0220 F0221 L00 M0223 D210 L01 M1020 F0222 F0223 E20
M1021 F1020 Q00 L02 D211 M1022 L03 F1021 M1023 F1022 E21 D220 M1220 D300 D330 D221 M1221 D331
M1222 D230 Q01 E22 Q02 F1023 E33 F1220 E23 M1223 F1221 L10 F1222 M2020 F1223 L11 D301 M2021 Q03
Q10 M2022 F2020 E30 F2021 L12 M2023 D310 L13 M2220 F2022 D311 Q11 M2221 Q12 Q13 p0 D320 M2222
E31 p1 D321 b0 b1 F2023 E32 F2220 M2223 L20 F2221 F2222 M3020 L21 F2223 W3i M3021 Q20 Q21 L22
M3022 M3023 L23 F3020 F3021 M3210 F3022 Q22 Q23 M3211 F3023 W3q M3212 F3210 L30 F3211 M3213
F3212 M3310 F3213 L31 M3311 F3310 M3312 F3311 Q30 M3313 Q31 F3312 L32 Z0 F3313 Z1 l0 Q32 l1 Z2
L33 l2 Q33 m0 Z3 m1 e0 m2 e1 l3 e2 r0 r1 o0 m3 o1 r2 e3 o2 r3 o3
"""


def tile_dqn_pa_kernel(tc, x, h1_bytes, h1_scale, W2, b2, W3, b3, out):
    nc = tc.nc
    with ExitStack() as ctx:
        keep = ctx.enter_context(tc.tile_pool(name="keep", bufs=1))
        rawp = ctx.enter_context(tc.tile_pool(name="rawp", bufs=RAWBUFS))
        wgp = ctx.enter_context(tc.tile_pool(name="wgp", bufs=6))
        hrp = ctx.enter_context(tc.tile_pool(name="hrp", bufs=2))
        hbp = ctx.enter_context(tc.tile_pool(name="hbp", bufs=6))
        xp = ctx.enter_context(tc.tile_pool(name="xp", bufs=2))
        hgp = ctx.enter_context(tc.tile_pool(name="hgp", bufs=2))
        vp = ctx.enter_context(tc.tile_pool(name="vp", bufs=3))
        h2p = ctx.enter_context(tc.tile_pool(name="h2p", bufs=5))
        smp = ctx.enter_context(tc.tile_pool(name="smp", bufs=1))
        mmp = ctx.enter_context(tc.psum_pool(name="mmp", bufs=4))
        trp = ctx.enter_context(tc.psum_pool(name="trp", bufs=2))
        axp = ctx.enter_context(tc.psum_pool(name="axp", bufs=2))
        ctx.enter_context(tc.manual_schedule())

        ident = keep.tile([P, P], F32, name="ident")
        identb = keep.tile([P, P], BF16, name="identb")
        h1b = {}
        sct = keep.tile([P, H1], F32, name="sct", align_bytes=64)
        h1c = keep.tile([P, 4, B], U32, name="h1c", align_bytes=256)
        h1s = keep.tile([P, 4, B], U8, name="h1s", align_bytes=256)
        w2c = keep.tile([P, 4, 4, 512], U32, name="w2c", align_bytes=256)
        w2s = keep.tile([P, 4, 4, 512], U8, name="w2s", align_bytes=256)
        h2c = keep.tile([P, 4, B], U32, name="h2c", align_bytes=256)
        h2s = keep.tile([P, 4, B], U8, name="h2s", align_bytes=256)
        w3c = keep.tile([P, 4 * A], U32, name="w3c", align_bytes=256)
        w3s = keep.tile([P, 4 * A], U8, name="w3s", align_bytes=256)
        b2r = keep.tile([P, P], BF16, name="b2r")
        b2c = keep.tile([P, 16], F32, name="b2c")
        b3t = keep.tile([P, A], BF16, name="b3t")
        pb = keep.tile([P, 8, A], F32, name="pb")
        dummy = keep.tile([P, 1], F32, name="dummy")

        raw = {}
        wg = {}
        hrow = {}
        tr = {}
        hg = {}
        mm = {}
        v = {}
        h2b = {}
        aux = {}
        sm = {}
        xts = {}
        w3 = {}

        def load_x(h):
            xts[h] = xp.tile([P, 4, A * G], BF16, name="xt", align_bytes=64)
            nc.sync.dma_start(out=xts[h][:], in_=x[512 * h : 512 * h + 512, :].rearrange("(n p) f -> p n f", p=P))

        def load_w2(g, c, part=None):
            if part in (None, 0):
                raw[g, c] = rawp.tile([P, 4, 512], BF16, name="raw", align_bytes=64)
            src = W2[512 * c : 512 * c + 512, 512 * g : 512 * g + 512].rearrange("(p j) n -> p j n", j=4)
            if part is not None:
                cols = slice(256 * part, 256 * part + 256)
                nc.sync.dma_start(out=raw[g, c][:, :, cols], in_=src[:, :, cols])
            else:
                nc.sync.dma_start(out=raw[g, c][:], in_=src)

        def load_h1(b):
            h1b[b] = hbp.tile([P, H1], U8, name="h1b", align_bytes=64)
            q = b // 2
            rows = h1_bytes[256 * q : 256 * q + 256, :].rearrange("(y j s) k -> j s y k", y=4, j=2)
            nc.sync.dma_start(out=h1b[b][:], in_=rows[b % 2])

        def op_D(g, c, k):
            if (g, c) not in wg:
                wg[g, c] = wgp.tile([P, 2048], BF16, name="wg", align_bytes=256)
            dst = wg[g, c][:].rearrange("p (t q r j) -> p t q r j", t=4, q=16, r=8)[:, :, 8 * k : 8 * k + 8, :, :]
            src = raw[g, c][:, :, 256 * k : 256 * k + 256].rearrange("p j (q t r) -> p t q r j", q=8, t=4)

            dst = dst.rearrange("p t q r j -> p t q j r")
            src = src.rearrange("p t q r j -> p t q j r")
            if "D%d%d%d" % (g, c, k) in ON_VECTOR:
                nc.vector.tensor_copy(out=dst, in_=src)
            else:
                nc.scalar.copy(out=dst, in_=src)

        def op_I(g, c, k):
            tr["I", g, c, k] = trp.tile([P, 1024], BF16, name="tr")
            dst = tr["I", g, c, k][:].rearrange("p (n j) -> p j n", j=4)
            src = raw[g, c][:].rearrange("p j (q t r) -> p j t q r", q=16, t=4)
            for j in range(4):
                nc.tensor.matmul(
                    dst[:, j, :].rearrange("p (t q r) -> p t q r", t=2, q=16),
                    lhsT=identb[:],
                    rhs=src[:, j, 2 * k : 2 * k + 2, :, :],
                    start=True,
                    stop=True,
                )

        def op_K(g, c, k):
            if (g, c) not in wg:
                wg[g, c] = wgp.tile([P, 2048], BF16, name="wg", align_bytes=256)
            dst = wg[g, c][:, 1024 * k : 1024 * k + 1024]
            if "D%d%d%d" % (g, c, k) in ON_VECTOR:
                nc.vector.tensor_copy(out=dst, in_=tr["I", g, c, k][:])
            else:
                nc.scalar.copy(out=dst, in_=tr["I", g, c, k][:])

        def op_E(g, c):
            nc.vector.quantize_mx(out=w2c[:, g, c, :].bitcast(X4), scales=w2s[:, g, c, :], in_=wg[g, c][:])

        def op_A(b, i=None):
            if b not in hrow:
                hrow[b] = hrp.tile([P, H1], BF16, name="hrow", align_bytes=64)
            sl = slice(0, H1) if i is None else slice(1024 * i, 1024 * i + 1024)
            nc.vector.tensor_tensor(out=hrow[b][:, sl], in0=h1b[b][:, sl].bitcast(FP8), in1=sct[:, sl], op=ALU.mult)

        def op_T(b, i):
            tr[b, i] = trp.tile([P, 2, 2, P], F32, name="tr")
            words = hrow[b][:].bitcast(F32)
            for cc in range(2):
                for u in range(2):
                    w0 = 256 * (2 * i + cc) + u
                    nc.tensor.transpose(tr[b, i][:, cc, u, :], words[:, w0 : 256 * (2 * i + cc + 1) : 2], ident[:])

        def op_B(b, i):
            q = b // 2
            if q not in hg:
                hg[q] = hgp.tile([P, 4, 1024], BF16, name="hg", align_bytes=256)
            o = (b % 2) * 256
            dst = hg[q][:].bitcast(F32)[:, 2 * i : 2 * i + 2, o : o + 256].rearrange("p c (r u) -> p c r u", u=2)
            nc.scalar.copy(out=dst, in_=tr[b, i][:].rearrange("p c u r -> p c r u"))

        def op_C(q, c):
            nc.vector.quantize_mx(
                out=h1c[:, c, 256 * q : 256 * q + 256].bitcast(X4),
                scales=h1s[:, c, 256 * q : 256 * q + 256],
                in_=hg[q][:, c, :],
            )

        def op_M(g, q, n, t):
            mm[g, q, t] = mmp.tile([P, 512], F32, name="mm")
            cols = slice(256 * q, 256 * (q + n))
            for c in range(4):
                nc.tensor.matmul_mx(
                    out=mm[g, q, t][:, 0 : 256 * n],
                    lhsT=w2c[:, g, c, P * t : P * t + P].bitcast(X4),
                    lhsT_scale=w2s[:, g, c, P * t : P * t + P],
                    rhs=h1c[:, c, cols].bitcast(X4),
                    rhs_scale=h1s[:, c, cols],
                    start=(c == 0),
                    stop=(c == 3),
                )

        def op_F(g, q, n, t):
            h = q // 2
            if (g, h) not in v:
                v[g, h] = vp.tile([P, 2, 64, 4, 4], F32, name="v", align_bytes=64)
            k = q - 2 * h
            nc.scalar.activation(
                out=v[g, h][:, k : k + n, :, t, :].rearrange("p k s y -> p (k s) y"),
                in_=mm[g, q, t][:, 0 : 256 * n].rearrange("p (s y) -> p s y", y=4),
                func=ACT.Identity,
                bias=b2c[:, 4 * g + t : 4 * g + t + 1],
                scale=1.0,
            )

        def op_L(g, q):
            h2b[g, q] = h2p.tile([P, 4, 64, 4], BF16, name="h2b", align_bytes=64)
            src = v[g, q // 2][:, q % 2, :, :, :].rearrange("p s t y -> p (s t) y")
            nc.vector.scalar_tensor_tensor(
                out=h2b[g, q][:].rearrange("p y s t -> p (s t) y"), in0=src, scalar=SLOPE, in1=src, op0=ALU.mult, op1=ALU.max
            )

        def op_Q(g, q):
            nc.vector.quantize_mx(
                out=h2c[:, g, 256 * q : 256 * q + 256].bitcast(X4),
                scales=h2s[:, g, 256 * q : 256 * q + 256],
                in_=h2b[g, q][:].rearrange("p y s t -> p (y s t)"),
            )

        def op_G(h):
            xt = xts[h]
            aux["g", h] = axp.tile([P, 4, A], F32, name="aux")
            xv = xt[:].rearrange("p n (a f) -> p n a f", f=G)
            for f in range(G):
                nc.tensor.matmul(
                    aux["g", h][:], lhsT=identb[:], rhs=xv[:, :, :, f], start=(f == 0), stop=(f == G - 1)
                )

        def op_p(h):
            nc.vector.tensor_scalar(
                out=pb[:, 4 * h : 4 * h + 4, :], in0=aux["g", h][:], scalar1=0.0, scalar2=-BIG, op0=ALU.is_equal, op1=ALU.mult
            )

        def op_b(h):
            nc.vector.tensor_tensor(
                out=pb[:, 4 * h : 4 * h + 4, :],
                in0=pb[:, 4 * h : 4 * h + 4, :],
                in1=b3t[:].unsqueeze(1).to_broadcast([P, 4, A]),
                op=ALU.add,
            )

        def op_Z(q):
            aux["z", q] = axp.tile([P, 2, A], F32, name="aux")
            for n in range(2):
                o = 256 * q + P * n
                for g in range(4):
                    nc.tensor.matmul_mx(
                        out=aux["z", q][:, n, :],
                        lhsT=h2c[:, g, o : o + P].bitcast(X4),
                        lhsT_scale=h2s[:, g, o : o + P],
                        rhs=w3c[:, A * g : A * g + A].bitcast(X4),
                        rhs_scale=w3s[:, A * g : A * g + A],
                        start=(g == 0),
                        stop=(g == 3),
                    )

        def op_l(q):
            sm["l", q] = smp.tile([P, 2, A], F32, name="lt%d" % q)
            nc.vector.tensor_tensor(out=sm["l", q][:], in0=aux["z", q][:], in1=pb[:, 2 * q : 2 * q + 2, :], op=ALU.add)

        def op_m(q):
            sm["m", q] = smp.tile([P, 2], F32, name="mx%d" % q)
            sm["n", q] = smp.tile([P, 2], F32, name="ng%d" % q)
            nc.vector.tensor_reduce(out=sm["m", q][:], in_=sm["l", q][:], axis=AX.X, op=ALU.max)
            nc.vector.tensor_scalar(out=sm["n", q][:], in0=sm["m", q][:], scalar1=-1.0, scalar2=None, op0=ALU.mult)

        def op_e(q):
            sm["e", q] = smp.tile([P, 2, A], F32, name="et%d" % q)
            sm["s", q] = smp.tile([P, 2], F32, name="su%d" % q)
            for n in range(2):
                nc.scalar.activation(
                    out=sm["e", q][:, n, :],
                    in_=sm["l", q][:, n, :],
                    func=ACT.Exp,
                    bias=sm["n", q][:, n : n + 1],
                    scale=1.0,
                    accum_out=sm["s", q][:, n : n + 1],
                )

        def op_r(q):
            sm["r", q] = smp.tile([P, 2], F32, name="rs%d" % q)
            nc.vector.reciprocal(out=sm["r", q][:], in_=sm["s", q][:])

        def op_o(q):
            ot = sm["l", q]
            for n in range(2):
                nc.scalar.activation(
                    out=ot[:, n, :], in_=sm["e", q][:, n, :], func=ACT.Copy, scale=sm["r", q][:, n : n + 1]
                )
            nc.sync.dma_start(out=out[256 * q : 256 * q + 256, :].rearrange("(n p) a -> p n a", p=P), in_=ot[:])

        def op_W3i():
            w3["g"] = wgp.tile([P, 2048], BF16, name="wg", align_bytes=256)
            nc.scalar.copy(
                out=w3["g"][:].rearrange("p (g a t) -> p g a t", g=4, t=4), in_=w3["r"][:].rearrange("p g (t a) -> p g a t", t=4)
            )

        def op_W3q():
            nc.vector.quantize_mx(out=w3c[:].bitcast(X4), scales=w3s[:], in_=w3["g"][:])

        nc.vector.memset(dummy[:], 0.0)
        nc.scalar.activation(out=dummy[:], in_=dummy[:], func=ACT.Exp)
        nc.vector.memset(b2r[:], 0.0)
        units = [(g, c) for g in range(4) for c in range(4)]

        def load_sc(i):
            nc.sync.dma_start(
                out=sct[:, 1024 * i : 1024 * i + 1024],
                in_=h1_scale.rearrange("o k -> (o k)")[1024 * i : 1024 * i + 1024].partition_broadcast(P),
            )

        def load_b2():
            for g in range(4):
                nc.sync.dma_start(
                    out=b2r[4 * g : 4 * g + 4, :].rearrange("t (q r) -> t q r", q=16),
                    in_=b2[512 * g : 512 * g + 512].rearrange("(q t r) -> t q r", q=16, t=4),
                )

        make_identity(nc, ident[:])
        make_identity(nc, identb[:])
        for name in "W000 W001 W01 S0 H0 S1 H1 W02 H2 b2 W03 H3 W10 H4 X0 X1 W11 H5 W12 b3".split():
            if name[0] == "W":
                load_w2(int(name[1]), int(name[2]), int(name[3]) if len(name) > 3 else None)
            elif name[0] == "S":
                load_sc(int(name[1]))
            elif name[0] == "H":
                load_h1(int(name[1]))
            elif name[0] == "X":
                load_x(int(name[1]))
            elif name == "b2":
                load_b2()
            elif name == "b3":
                nc.sync.dma_start(out=b3t[:], in_=b3.partition_broadcast(P))

        def load_w3():
            w3["r"] = rawp.tile([P, 4, 512], BF16, name="raw", align_bytes=64)
            for g in range(4):
                for t in range(4):
                    nc.sync.dma_start(
                        out=w3["r"][:, g, A * t : A * t + A],
                        in_=W3[512 * g : 512 * g + 512, :].rearrange("(q t r) a -> t q r a", q=16, t=4)[t],
                    )

        nxt = RAWBUFS
        seen = {}
        for name in ORDER.split():
            if name in ("W3i", "W3q"):
                if name == "W3i":
                    op_W3i()
                else:
                    op_W3q()
                continue
            kind = name[0]
            rest = name[1:].replace("_", "")
            args = [int(ch) for ch in rest]
            if kind == "F" and "b2" not in seen:
                seen["b2"] = 1
            if kind in "DI":
                (op_D if kind == "D" else op_I)(*args)
                key = (args[0], args[1])
                seen[key] = seen.get(key, 0) + 1
                while nxt < 17 and seen.get(divmod(nxt - RAWBUFS, 4), 0) == 2:
                    if nxt < 16:
                        load_w2(*units[nxt])
                    else:
                        load_w3()
                    nxt += 1
            elif kind == "K":
                op_K(*args)
            elif kind == "A":
                op_A(*args)
                seen["A", args[0]] = seen.get(("A", args[0]), 0) + (3 - len(args))
                if args[0] < 2 and seen["A", args[0]] == 2:
                    load_h1(args[0] + 6)
            elif kind == "T":
                op_T(*args)
                if args == [1, 0]:
                    bp = axp.tile([P, P], BF16, name="aux")
                    nc.tensor.transpose(bp[:], b2r[:], identb[:])
            elif kind == "B":
                op_B(*args)
                if args == [1, 1]:
                    nc.scalar.copy(out=b2c[:], in_=bp[:, 0:16])
            elif kind == "C":
                op_C(*args)
            elif kind == "E":
                op_E(*args)
            elif kind == "M":
                op_M(*args)
            elif kind == "F":
                op_F(*args)
            elif kind == "L":
                op_L(*args)
            elif kind == "Q":
                op_Q(*args)
            elif kind == "G":
                op_G(*args)
            elif kind == "p":
                op_p(*args)
            elif kind == "b":
                op_b(*args)
            elif kind == "Z":
                op_Z(*args)
            elif kind == "l":
                op_l(*args)
            elif kind == "m":
                op_m(*args)
            elif kind == "e":
                op_e(*args)
            elif kind == "r":
                op_r(*args)
            elif kind == "o":
                op_o(*args)
